import numpy as np
import ml_dtypes


def mxq(x, axis, fmt="e4m3"):
    dtype, down = {"e4m3": (ml_dtypes.float8_e4m3fn, 7), "e5m2": (ml_dtypes.float8_e5m2, 14)}[fmt]
    v = np.moveaxis(np.asarray(x, np.float32).astype(ml_dtypes.bfloat16).astype(np.float64), axis, -1)
    blocks = v.reshape(v.shape[:-1] + (-1, 32))
    amax = np.abs(blocks).max(-1, keepdims=True)
    byte = np.maximum(np.where(amax > 0, np.frexp(amax)[1] - 1 + 127, 0) - down, 1)
    scale = np.exp2(byte - 127.0)
    codes = (blocks / scale).astype(np.float32).astype(dtype).astype(np.float64)
    return np.moveaxis((codes * scale).reshape(v.shape), -1, axis)


WIDE = False


def mx_kscale(k):
    if not WIDE:
        return np.ones(k)
    levels = np.array([10, -10, 5, -5, 0])
    a = np.random.permutation(np.resize(levels, k // 512 * 4)).reshape(k // 512, 4)
    idx = np.arange(k)
    return np.exp2(a[idx // 512, idx % 128 // 32])


BF16 = ml_dtypes.bfloat16


def bf(x):
    return np.asarray(x, np.float32).astype(BF16)


def f64(x):
    return np.asarray(x).astype(np.float64)


B, C, D, H, W, W0, W1 = 16, 512, 128, 16, 32, 32, 256
N = H * W


def setup_inputs():
    s = mx_kscale(C)
    idx = np.arange(N)
    band = np.abs(idx[:, None] - idx[None, :]) <= W0
    return {
        "x": bf(np.random.standard_normal((B, C, N)) * s[None, :, None]),
        "q": bf(np.random.standard_normal((B, N, D)) * 0.42),
        "k": bf(np.random.standard_normal((B, D, N)) * 0.42),
        "mask0": bf(np.where(band, 0.3 * np.random.standard_normal((N, N)), -1e9)),
        "wv0": bf(np.random.standard_normal((C, C)) * 1.0 / np.sqrt(C) / s[None, :]),
        "bv0": bf(np.random.standard_normal(C) * 0.3),
    }


def reference(x, q, k, mask0, wv0, bv0):
    val = (mxq(f64(wv0), 1, "e4m3") @ mxq(f64(x), 1, "e4m3")) + f64(bv0)[None, :, None]
    s = f64(q) @ f64(k) + f64(mask0)[None]
    e = np.exp(s - s.max(-1, keepdims=True))
    return (mxq(val, 2, "e4m3") @ mxq(e, 2, "e4m3").transpose(0, 2, 1)) / e.sum(-1)[:, None, :]

@@ -1,0 +1,172 @@
+from contextlib import ExitStack
+
+import concourse.mybir as mybir
+from concourse.masks import make_identity
+
+BF16 = mybir.dt.bfloat16
+F32 = mybir.dt.float32
+U32 = mybir.dt.uint32
+U8 = mybir.dt.uint8
+FP8X4 = mybir.dt.float8_e4m3fn_x4
+ACT = mybir.ActivationFunctionType
+ALU = mybir.AluOpType
+AXIS = mybir.AxisListType
+
+P = 128
+PACK = 4
+BATCH, CH, HEAD, POS = 16, 512, 128, 512
+TILES = POS // P
+
+FLOPS = BATCH * (2 * CH * CH * POS + 2 * POS * HEAD * POS + 2 * CH * POS * POS)
+
+
+def quantise(nc, grouped, codes, scales):
+    nc.vector.quantize_mx(
+        out=codes[:].bitcast(FP8X4),
+        scales=scales[:],
+        in_=grouped[:].rearrange("p w j -> p (w j)"),
+    )
+
+
+def mx_operand(pool, width, name):
+    codes = pool.tile([P, width], U32, name=name + "_codes", align_bytes=64)
+    scales = pool.tile([P, width], U8, name=name + "_scales", align_bytes=64)
+    return codes, scales
+
+
+def tile_mvpam_module_mask_cascade_pa_t_kernel(tc, x, q, k, mask0, wv0, bv0, out):
+    nc = tc.nc
+    with ExitStack() as ctx:
+        const = ctx.enter_context(tc.tile_pool(name="const", bufs=1))
+        load = ctx.enter_context(tc.tile_pool(name="load", bufs=3))
+        work = ctx.enter_context(tc.tile_pool(name="work", bufs=2))
+        store = ctx.enter_context(tc.tile_pool(name="store", bufs=4))
+        psum = ctx.enter_context(tc.psum_pool(name="psum", bufs=2))
+
+        ident_bf = const.tile([P, P], BF16)
+        make_identity(nc, ident_bf[:])
+        ident_f32 = const.tile([P, P], F32)
+        make_identity(nc, ident_f32[:])
+
+        w_rows = const.tile([P, TILES, CH], BF16)
+        nc.sync.dma_start(out=w_rows[:], in_=wv0.rearrange("(g p) k -> p g k", p=P))
+        mask_rows = const.tile([P, TILES, POS], BF16)
+        nc.scalar.dma_start(out=mask_rows[:], in_=mask0.rearrange("(i p) n -> p i n", p=P))
+        bias_all = const.tile([P, CH], BF16)
+        nc.scalar.dma_start(out=bias_all[:], in_=bv0.partition_broadcast(P))
+
+        w_grouped = const.tile([P, CH, PACK], BF16, align_bytes=64)
+        for g in range(TILES):
+            w_t = psum.tile([P, PACK, P], BF16, tag="tr")
+            for t in range(PACK):
+                nc.tensor.transpose(w_t[:, t, :], w_rows[:, g, t * P : (t + 1) * P], ident_bf[:])
+            nc.vector.tensor_copy(
+                out=w_grouped[:, g * P : (g + 1) * P, :], in_=w_t[:].rearrange("p t c -> p c t")
+            )
+        w_codes, w_scales = mx_operand(const, CH, "w")
+        quantise(nc, w_grouped, w_codes, w_scales)
+
+        for b in range(BATCH):
+            x_rows = load.tile([P, PACK, POS], BF16)
+            nc.sync.dma_start(out=x_rows[:], in_=x[b].rearrange("(t p) n -> p t n", p=P))
+            q_rows = load.tile([P, TILES, HEAD], BF16)
+            nc.sync.dma_start(out=q_rows[:], in_=q[b].rearrange("(i p) d -> p i d", p=P))
+            k_rows = load.tile([P, POS], BF16)
+            nc.sync.dma_start(out=k_rows[:], in_=k[b])
+
+            x_grouped = work.tile([P, POS, PACK], BF16, align_bytes=64)
+            nc.scalar.copy(
+                out=x_grouped[:].rearrange("p (c i) t -> p c t i", i=4),
+                in_=x_rows[:].rearrange("p t (c i) -> p c t i", i=4),
+            )
+            x_codes, x_scales = mx_operand(work, POS, "x")
+            quantise(nc, x_grouped, x_codes, x_scales)
+
+            q_t = psum.tile([P, TILES, P], BF16, tag="tr")
+            for i in range(TILES):
+                nc.tensor.transpose(q_t[:, i, :], q_rows[:, i, :], ident_bf[:])
+            q_cols = work.tile([P, POS], BF16)
+            nc.scalar.copy(out=q_cols[:], in_=q_t[:].rearrange("p i m -> p (i m)"))
+
+            v_grouped = work.tile([P, CH, PACK], BF16, align_bytes=64)
+            for g in range(TILES):
+                chans = slice(g * P, (g + 1) * P)
+                v_acc = psum.tile([P, PACK, P], F32, tag="val")
+                for t in range(PACK):
+                    keys = slice(t * P, (t + 1) * P)
+                    nc.tensor.matmul_mx(
+                        out=v_acc[:, t, :],
+                        lhsT=x_codes[:, keys].bitcast(FP8X4),
+                        lhsT_scale=x_scales[:, keys],
+                        rhs=w_codes[:, chans].bitcast(FP8X4),
+                        rhs_scale=w_scales[:, chans],
+                        start=True,
+                        stop=True,
+                    )
+                nc.vector.tensor_tensor(
+                    out=v_grouped[:, chans, :],
+                    in0=v_acc[:].rearrange("p t c -> p c t"),
+                    in1=bias_all[:, chans].unsqueeze(2).to_broadcast([P, P, PACK]),
+                    op=ALU.add,
+                )
+            v_codes, v_scales = mx_operand(work, CH, "v")
+            quantise(nc, v_grouped, v_codes, v_scales)
+
+            neg_max = work.tile([P, TILES], F32)
+            row_sum = work.tile([P, TILES], F32)
+            e_rows = work.tile([P, TILES, POS], BF16)
+            for i in range(TILES):
+                s_acc = psum.tile([P, POS], F32, tag="s")
+                nc.tensor.matmul(
+                    s_acc[:], lhsT=q_cols[:, i * P : (i + 1) * P], rhs=k_rows[:], start=True, stop=True
+                )
+                s_rows = work.tile([P, POS], F32)
+                nc.vector.tensor_tensor(out=s_rows[:], in0=s_acc[:], in1=mask_rows[:, i, :], op=ALU.add)
+                nc.vector.tensor_reduce(
+                    out=neg_max[:, i : i + 1], in_=s_rows[:], axis=AXIS.X, op=ALU.max, negate=True
+                )
+                nc.scalar.activation(
+                    out=e_rows[:, i, :],
+                    in_=s_rows[:],
+                    func=ACT.Exp,
+                    bias=neg_max[:, i : i + 1],
+                    scale=1.0,
+                    accum_out=row_sum[:, i : i + 1],
+                )
+
+            e_grouped = work.tile([P, POS, PACK], BF16, align_bytes=64)
+            for i in range(TILES):
+                e_t = psum.tile([P, PACK, P], BF16, tag="tr")
+                for t in range(PACK):
+                    nc.tensor.transpose(e_t[:, t, :], e_rows[:, i, t * P : (t + 1) * P], ident_bf[:])
+                nc.scalar.copy(
+                    out=e_grouped[:, i * P : (i + 1) * P, :], in_=e_t[:].rearrange("p t m -> p m t")
+                )
+            e_codes, e_scales = mx_operand(work, POS, "e")
+            quantise(nc, e_grouped, e_codes, e_scales)
+
+            recip = work.tile([P, TILES], F32)
+            nc.vector.reciprocal(out=recip[:], in_=row_sum[:])
+            r_t = psum.tile([P, POS], F32, tag="tr")
+            for i in range(TILES):
+                nc.tensor.transpose(
+                    r_t[:, i * P : (i + 1) * P], recip[:, i : i + 1].to_broadcast([P, P]), ident_f32[:]
+                )
+            recip_all = work.tile([P, POS], F32)
+            nc.scalar.copy(out=recip_all[:], in_=r_t[:])
+
+            for g in range(TILES):
+                chans = slice(g * P, (g + 1) * P)
+                o_acc = psum.tile([P, POS], F32, tag="o")
+                nc.tensor.matmul_mx(
+                    out=o_acc[:],
+                    lhsT=v_codes[:, chans].bitcast(FP8X4),
+                    lhsT_scale=v_scales[:, chans],
+                    rhs=e_codes[:].bitcast(FP8X4),
+                    rhs_scale=e_scales[:],
+                    start=True,
+                    stop=True,
+                )
+                o_rows = store.tile([P, POS], F32)
+                nc.vector.tensor_tensor(out=o_rows[:], in0=o_acc[:], in1=recip_all[:], op=ALU.mult)
+                nc.sync.dma_start(out=out[b, chans, :], in_=o_rows[:])

@@ -16,11 +16,28 @@ P = 128
 PACK = 4
 BATCH, CH, HEAD, POS = 16, 512, 128, 512
 TILES = POS // P
+BAND = 32
+
+WINDOW = P + 2 * BAND
+SHIFT = P // 2
+MARGIN = SHIFT - BAND
 
 FLOPS = BATCH * (2 * CH * CH * POS + 2 * POS * HEAD * POS + 2 * CH * POS * POS)
 
 
-def quantise(nc, grouped, codes, scales):
+def cyclic_pieces(start, width, period):
+    pieces = []
+    offset = 0
+    while offset < width:
+        first = (start + offset) % period
+        length = min(width - offset, period - first)
+        pieces.append((offset, first, first + length))
+        offset += length
+    return pieces
+
+
+def quantise(nc, grouped, operand):
+    codes, scales = operand
     nc.vector.quantize_mx(
         out=codes[:].bitcast(FP8X4),
         scales=scales[:],
@@ -34,139 +51,220 @@ def mx_operand(pool, width, name):
     return codes, scales
 
 
+def mx_pass(nc, acc, stationary, stationary_cols, moving, moving_cols):
+    nc.tensor.matmul_mx(
+        out=acc,
+        lhsT=stationary[0][:, stationary_cols].bitcast(FP8X4),
+        lhsT_scale=stationary[1][:, stationary_cols],
+        rhs=moving[0][:, moving_cols].bitcast(FP8X4),
+        rhs_scale=moving[1][:, moving_cols],
+        start=True,
+        stop=True,
+    )
+
+
+def tile_cols(i):
+    return slice(i * P, (i + 1) * P)
+
+
 def tile_mvpam_module_mask_cascade_pa_t_kernel(tc, x, q, k, mask0, wv0, bv0, out):
     nc = tc.nc
     with ExitStack() as ctx:
+        ctx.enter_context(tc.manual_schedule())
         const = ctx.enter_context(tc.tile_pool(name="const", bufs=1))
         load = ctx.enter_context(tc.tile_pool(name="load", bufs=3))
         work = ctx.enter_context(tc.tile_pool(name="work", bufs=2))
-        store = ctx.enter_context(tc.tile_pool(name="store", bufs=4))
+        store = ctx.enter_context(tc.tile_pool(name="store", bufs=6))
         psum = ctx.enter_context(tc.psum_pool(name="psum", bufs=2))
+
+        live = {}
+
+        def load_inputs(b):
+            x_rows = load.tile([P, PACK, POS], BF16)
+            for offset, first, end in cyclic_pieces(-SHIFT, POS, POS):
+                nc.sync.dma_start(
+                    out=x_rows[:, :, offset : offset + end - first],
+                    in_=x[b, :, first:end].rearrange("(t p) n -> p t n", p=P),
+                )
+            q_rows = load.tile([P, TILES, HEAD], BF16)
+            nc.sync.dma_start(out=q_rows[:], in_=q[b].rearrange("(i p) d -> p i d", p=P))
+            k_rows = load.tile([P, POS], BF16)
+            nc.sync.dma_start(out=k_rows[:], in_=k[b])
+            live["x_rows", b], live["q_rows", b], live["k_rows", b] = x_rows, q_rows, k_rows
+
+        w_rows = const.tile([P, TILES, CH], BF16)
+        nc.sync.dma_start(out=w_rows[:], in_=wv0.rearrange("(g p) k -> p g k", p=P))
+        load_inputs(0)
+        mask_win = const.tile([P, TILES, WINDOW], BF16)
+        for i in range(TILES):
+            for offset, first, end in cyclic_pieces(i * P - BAND, WINDOW, POS):
+                nc.scalar.dma_start(
+                    out=mask_win[:, i, offset : offset + end - first],
+                    in_=mask0[tile_cols(i), first:end],
+                )
+        bias_all = const.tile([P, CH], BF16)
+        nc.scalar.dma_start(out=bias_all[:], in_=bv0.partition_broadcast(P))
 
         ident_bf = const.tile([P, P], BF16)
         make_identity(nc, ident_bf[:])
         ident_f32 = const.tile([P, P], F32)
         make_identity(nc, ident_f32[:])
 
-        w_rows = const.tile([P, TILES, CH], BF16)
-        nc.sync.dma_start(out=w_rows[:], in_=wv0.rearrange("(g p) k -> p g k", p=P))
-        mask_rows = const.tile([P, TILES, POS], BF16)
-        nc.scalar.dma_start(out=mask_rows[:], in_=mask0.rearrange("(i p) n -> p i n", p=P))
-        bias_all = const.tile([P, CH], BF16)
-        nc.scalar.dma_start(out=bias_all[:], in_=bv0.partition_broadcast(P))
+        e_win = [const.tile([P, TILES, 2 * P], BF16, name="e_win%d" % h) for h in range(2)]
+        e_grouped = [
+            const.tile([P, POS, PACK], BF16, name="e_grouped%d" % h, align_bytes=64) for h in range(2)
+        ]
+        for h in range(2):
+            nc.vector.memset(e_win[h][:], 0.0)
+            nc.vector.memset(e_grouped[h][:], 0.0)
 
         w_grouped = const.tile([P, CH, PACK], BF16, align_bytes=64)
         for g in range(TILES):
             w_t = psum.tile([P, PACK, P], BF16, tag="tr")
             for t in range(PACK):
-                nc.tensor.transpose(w_t[:, t, :], w_rows[:, g, t * P : (t + 1) * P], ident_bf[:])
+                nc.tensor.transpose(w_t[:, t, :], w_rows[:, g, tile_cols(t)], ident_bf[:])
             nc.vector.tensor_copy(
-                out=w_grouped[:, g * P : (g + 1) * P, :], in_=w_t[:].rearrange("p t c -> p c t")
+                out=w_grouped[:, tile_cols(g), :], in_=w_t[:].rearrange("p t c -> p c t")
             )
-        w_codes, w_scales = mx_operand(const, CH, "w")
-        quantise(nc, w_grouped, w_codes, w_scales)
+        w_mx = mx_operand(const, CH, "w")
+        quantise(nc, w_grouped, w_mx)
 
-        for b in range(BATCH):
-            x_rows = load.tile([P, PACK, POS], BF16)
-            nc.sync.dma_start(out=x_rows[:], in_=x[b].rearrange("(t p) n -> p t n", p=P))
-            q_rows = load.tile([P, TILES, HEAD], BF16)
-            nc.sync.dma_start(out=q_rows[:], in_=q[b].rearrange("(i p) d -> p i d", p=P))
-            k_rows = load.tile([P, POS], BF16)
-            nc.sync.dma_start(out=k_rows[:], in_=k[b])
-
+        def group_x(b):
             x_grouped = work.tile([P, POS, PACK], BF16, align_bytes=64)
             nc.scalar.copy(
                 out=x_grouped[:].rearrange("p (c i) t -> p c t i", i=4),
-                in_=x_rows[:].rearrange("p t (c i) -> p c t i", i=4),
+                in_=live["x_rows", b][:].rearrange("p t (c i) -> p c t i", i=4),
             )
-            x_codes, x_scales = mx_operand(work, POS, "x")
-            quantise(nc, x_grouped, x_codes, x_scales)
+            live["x_grouped", b] = x_grouped
 
+        def quantise_x(b):
+            live["x_mx", b] = mx_operand(work, POS, "x")
+            quantise(nc, live["x_grouped", b], live["x_mx", b])
+
+        def transpose_q(b):
+            q_rows = live["q_rows", b]
             q_t = psum.tile([P, TILES, P], BF16, tag="tr")
             for i in range(TILES):
                 nc.tensor.transpose(q_t[:, i, :], q_rows[:, i, :], ident_bf[:])
             q_cols = work.tile([P, POS], BF16)
             nc.scalar.copy(out=q_cols[:], in_=q_t[:].rearrange("p i m -> p (i m)"))
+            live["q_cols", b] = q_cols
 
-            v_grouped = work.tile([P, CH, PACK], BF16, align_bytes=64)
-            for g in range(TILES):
-                chans = slice(g * P, (g + 1) * P)
-                v_acc = psum.tile([P, PACK, P], F32, tag="val")
-                for t in range(PACK):
-                    keys = slice(t * P, (t + 1) * P)
-                    nc.tensor.matmul_mx(
-                        out=v_acc[:, t, :],
-                        lhsT=x_codes[:, keys].bitcast(FP8X4),
-                        lhsT_scale=x_scales[:, keys],
-                        rhs=w_codes[:, chans].bitcast(FP8X4),
-                        rhs_scale=w_scales[:, chans],
-                        start=True,
-                        stop=True,
-                    )
-                nc.vector.tensor_tensor(
-                    out=v_grouped[:, chans, :],
-                    in0=v_acc[:].rearrange("p t c -> p c t"),
-                    in1=bias_all[:, chans].unsqueeze(2).to_broadcast([P, P, PACK]),
-                    op=ALU.add,
-                )
-            v_codes, v_scales = mx_operand(work, CH, "v")
-            quantise(nc, v_grouped, v_codes, v_scales)
-
+        def softmax_numerator(b):
+            q_cols, k_rows = live["q_cols", b], live["k_rows", b]
             neg_max = work.tile([P, TILES], F32)
             row_sum = work.tile([P, TILES], F32)
-            e_rows = work.tile([P, TILES, POS], BF16)
-            for i in range(TILES):
-                s_acc = psum.tile([P, POS], F32, tag="s")
-                nc.tensor.matmul(
-                    s_acc[:], lhsT=q_cols[:, i * P : (i + 1) * P], rhs=k_rows[:], start=True, stop=True
-                )
-                s_rows = work.tile([P, POS], F32)
-                nc.vector.tensor_tensor(out=s_rows[:], in0=s_acc[:], in1=mask_rows[:, i, :], op=ALU.add)
+            for pair in range(TILES // 2):
+                s_acc = psum.tile([P, 2, WINDOW], F32, tag="s")
+                for h in range(2):
+                    i = 2 * pair + h
+                    start_key = i * P - BAND
+                    first, end = max(start_key, 0), min(start_key + WINDOW, POS)
+                    nc.tensor.matmul(
+                        s_acc[:, h, :], lhsT=ident_bf[:], rhs=mask_win[:, i, :], start=True, stop=False
+                    )
+                    nc.tensor.matmul(
+                        s_acc[:, h, first - start_key : end - start_key],
+                        lhsT=q_cols[:, tile_cols(i)],
+                        rhs=k_rows[:, first:end],
+                        start=False,
+                        stop=True,
+                    )
                 nc.vector.tensor_reduce(
-                    out=neg_max[:, i : i + 1], in_=s_rows[:], axis=AXIS.X, op=ALU.max, negate=True
+                    out=neg_max[:, 2 * pair : 2 * pair + 2], in_=s_acc[:], axis=AXIS.X, op=ALU.max, negate=True
                 )
-                nc.scalar.activation(
-                    out=e_rows[:, i, :],
-                    in_=s_rows[:],
-                    func=ACT.Exp,
-                    bias=neg_max[:, i : i + 1],
-                    scale=1.0,
-                    accum_out=row_sum[:, i : i + 1],
-                )
+                for h in range(2):
+                    i = 2 * pair + h
+                    nc.scalar.activation(
+                        out=e_win[b % 2][:, i, MARGIN : MARGIN + WINDOW],
+                        in_=s_acc[:, h, :],
+                        func=ACT.Exp,
+                        bias=neg_max[:, i : i + 1],
+                        scale=1.0,
+                        accum_out=row_sum[:, i : i + 1],
+                    )
+            live["row_sum", b] = row_sum
 
-            e_grouped = work.tile([P, POS, PACK], BF16, align_bytes=64)
-            for i in range(TILES):
-                e_t = psum.tile([P, PACK, P], BF16, tag="tr")
+        def values(b):
+            x_mx = live["x_mx", b]
+            v_grouped = work.tile([P, CH, PACK], BF16, align_bytes=64)
+            for g in range(TILES):
+                v_acc = psum.tile([P, PACK, P], F32, tag="acc", bufs=4)
                 for t in range(PACK):
-                    nc.tensor.transpose(e_t[:, t, :], e_rows[:, i, t * P : (t + 1) * P], ident_bf[:])
-                nc.scalar.copy(
-                    out=e_grouped[:, i * P : (i + 1) * P, :], in_=e_t[:].rearrange("p t m -> p m t")
+                    mx_pass(nc, v_acc[:, t, :], x_mx, tile_cols(t), w_mx, tile_cols(g))
+                nc.vector.tensor_tensor(
+                    out=v_grouped[:, tile_cols(g), :],
+                    in0=v_acc[:].rearrange("p t c -> p c t"),
+                    in1=bias_all[:, tile_cols(g)].unsqueeze(2).to_broadcast([P, P, PACK]),
+                    op=ALU.add,
                 )
-            e_codes, e_scales = mx_operand(work, POS, "e")
-            quantise(nc, e_grouped, e_codes, e_scales)
+            live["v_grouped", b] = v_grouped
 
+        def quantise_values(b):
+            live["v_mx", b] = mx_operand(work, CH, "v")
+            quantise(nc, live["v_grouped", b], live["v_mx", b])
+
+        def transpose_e(b):
+            e_t = psum.tile([P, TILES, 2, P], BF16, tag="tr")
+            planes = [sorted(((i, 0), ((i + 1) % TILES, 1))) for i in range(TILES)]
+            for i in range(TILES):
+                for u in range(2):
+                    half = planes[i][u][1]
+                    nc.tensor.transpose(e_t[:, i, u, :], e_win[b % 2][:, i, tile_cols(half)], ident_bf[:])
+            for i in range(TILES):
+                low, high = planes[i][0][0], planes[i][1][0]
+                nc.scalar.copy(
+                    out=e_grouped[b % 2][:, tile_cols(i), low : high + 1 : high - low],
+                    in_=e_t[:, i, :, :].rearrange("p u m -> p m u"),
+                )
+
+        def quantise_e(b):
+            live["e_mx", b] = mx_operand(work, POS, "e")
+            quantise(nc, e_grouped[b % 2], live["e_mx", b])
+
+        def reciprocal_sums(b):
             recip = work.tile([P, TILES], F32)
-            nc.vector.reciprocal(out=recip[:], in_=row_sum[:])
+            nc.vector.reciprocal(out=recip[:], in_=live["row_sum", b][:])
+            live["recip", b] = recip
+
+        def spread_reciprocals(b):
+            recip = live["recip", b]
             r_t = psum.tile([P, POS], F32, tag="tr")
             for i in range(TILES):
-                nc.tensor.transpose(
-                    r_t[:, i * P : (i + 1) * P], recip[:, i : i + 1].to_broadcast([P, P]), ident_f32[:]
-                )
+                nc.tensor.transpose(r_t[:, tile_cols(i)], recip[:, i : i + 1].to_broadcast([P, P]), ident_f32[:])
             recip_all = work.tile([P, POS], F32)
             nc.scalar.copy(out=recip_all[:], in_=r_t[:])
+            live["recip_all", b] = recip_all
 
+        def result(b):
+            v_mx, e_mx, recip_all = live["v_mx", b], live["e_mx", b], live["recip_all", b]
             for g in range(TILES):
-                chans = slice(g * P, (g + 1) * P)
-                o_acc = psum.tile([P, POS], F32, tag="o")
-                nc.tensor.matmul_mx(
-                    out=o_acc[:],
-                    lhsT=v_codes[:, chans].bitcast(FP8X4),
-                    lhsT_scale=v_scales[:, chans],
-                    rhs=e_codes[:].bitcast(FP8X4),
-                    rhs_scale=e_scales[:],
-                    start=True,
-                    stop=True,
-                )
+                o_acc = psum.tile([P, POS], F32, tag="acc", bufs=4)
+                mx_pass(nc, o_acc[:], v_mx, tile_cols(g), e_mx, slice(0, POS))
                 o_rows = store.tile([P, POS], F32)
                 nc.vector.tensor_tensor(out=o_rows[:], in0=o_acc[:], in1=recip_all[:], op=ALU.mult)
-                nc.sync.dma_start(out=out[b, chans, :], in_=o_rows[:])
+                nc.sync.dma_start(out=out[b, tile_cols(g), :], in_=o_rows[:])
+
+        for j in range(BATCH + 2):
+            front, middle, end_item = j, j - 1, j - 2
+            if front + 1 < BATCH:
+                load_inputs(front + 1)
+            if 0 <= end_item:
+                result(end_item)
+            if 0 <= middle < BATCH:
+                reciprocal_sums(middle)
+                values(middle)
+            if front < BATCH:
+                group_x(front)
+                quantise_x(front)
+            if 0 <= middle < BATCH:
+                quantise_values(middle)
+            if front < BATCH:
+                transpose_q(front)
+            if 0 <= middle < BATCH:
+                transpose_e(middle)
+                spread_reciprocals(middle)
+            if front < BATCH:
+                softmax_numerator(front)
+            if 0 <= middle < BATCH:
+                quantise_e(middle)

@@ -249,11 +249,11 @@ def tile_mvpam_module_mask_cascade_pa_t_kernel(tc, x, q, k, mask0, wv0, bv0, out
             front, middle, end_item = j, j - 1, j - 2
             if front + 1 < BATCH:
                 load_inputs(front + 1)
+            if 0 <= middle < BATCH:
+                values(middle)
+                reciprocal_sums(middle)
             if 0 <= end_item:
                 result(end_item)
-            if 0 <= middle < BATCH:
-                reciprocal_sums(middle)
-                values(middle)
             if front < BATCH:
                 group_x(front)
                 quantise_x(front)

@@ -18,9 +18,12 @@ BATCH, CH, HEAD, POS = 16, 512, 128, 512
 TILES = POS // P
 BAND = 32
 
-WINDOW = P + 2 * BAND
-SHIFT = P // 2
-MARGIN = SHIFT - BAND
+GROUP = 64
+WINDOW = GROUP + 2 * BAND
+HALVES = 2
+PAIRS = WINDOW // 2
+MARGIN = P - 16
+E_WORDS = MARGIN + TILES * (PAIRS + MARGIN)
 
 FLOPS = BATCH * (2 * CH * CH * POS + 2 * POS * HEAD * POS + 2 * CH * POS * POS)
 
@@ -67,6 +70,10 @@ def tile_cols(i):
     return slice(i * P, (i + 1) * P)
 
 
+def window_word(i):
+    return MARGIN + i * (PAIRS + MARGIN)
+
+
 def tile_mvpam_module_mask_cascade_pa_t_kernel(tc, x, q, k, mask0, wv0, bv0, out):
     nc = tc.nc
     with ExitStack() as ctx:
@@ -81,11 +88,7 @@ def tile_mvpam_module_mask_cascade_pa_t_kernel(tc, x, q, k, mask0, wv0, bv0, out
 
         def load_inputs(b):
             x_rows = load.tile([P, PACK, POS], BF16)
-            for offset, first, end in cyclic_pieces(-SHIFT, POS, POS):
-                nc.sync.dma_start(
-                    out=x_rows[:, :, offset : offset + end - first],
-                    in_=x[b, :, first:end].rearrange("(t p) n -> p t n", p=P),
-                )
+            nc.sync.dma_start(out=x_rows[:], in_=x[b].rearrange("(t p) n -> p t n", p=P))
             q_rows = load.tile([P, TILES, HEAD], BF16)
             nc.sync.dma_start(out=q_rows[:], in_=q[b].rearrange("(i p) d -> p i d", p=P))
             k_rows = load.tile([P, POS], BF16)
@@ -97,11 +100,13 @@ def tile_mvpam_module_mask_cascade_pa_t_kernel(tc, x, q, k, mask0, wv0, bv0, out
         load_inputs(0)
         mask_win = const.tile([P, TILES, WINDOW], BF16)
         for i in range(TILES):
-            for offset, first, end in cyclic_pieces(i * P - BAND, WINDOW, POS):
-                nc.scalar.dma_start(
-                    out=mask_win[:, i, offset : offset + end - first],
-                    in_=mask0[tile_cols(i), first:end],
-                )
+            for h in range(HALVES):
+                g = i + TILES * h
+                for offset, first, end in cyclic_pieces(g * GROUP - BAND, WINDOW, POS):
+                    nc.scalar.dma_start(
+                        out=mask_win[h * GROUP : (h + 1) * GROUP, i, offset : offset + end - first],
+                        in_=mask0[g * GROUP : (g + 1) * GROUP, first:end],
+                    )
         bias_all = const.tile([P, CH], BF16)
         nc.scalar.dma_start(out=bias_all[:], in_=bv0.partition_broadcast(P))
 
@@ -110,17 +115,26 @@ def tile_mvpam_module_mask_cascade_pa_t_kernel(tc, x, q, k, mask0, wv0, bv0, out
         ident_f32 = const.tile([P, P], F32)
         make_identity(nc, ident_f32[:])
 
-        e_win = [const.tile([P, TILES, 2 * P], BF16, name="e_win%d" % h) for h in range(2)]
-        e_grouped = [
-            const.tile([P, POS, PACK], BF16, name="e_grouped%d" % h, align_bytes=64) for h in range(2)
-        ]
+        e_win = [const.tile([P, 2 * E_WORDS], BF16, name="e_win%d" % h) for h in range(2)]
+        q_wide = [const.tile([P, TILES, 3, GROUP], BF16, name="q_wide%d" % h) for h in range(2)]
         for h in range(2):
             nc.vector.memset(e_win[h][:], 0.0)
-            nc.vector.memset(e_grouped[h][:], 0.0)
+            nc.gpsimd.memset(q_wide[h][:], 0.0)
+        e_bank = [
+            psum.tile([P, 2, HALVES, 2, GROUP], F32, name="e_bank%d" % c, bufs=1) for c in range(2)
+        ]
+        for c in range(2):
+            for i in range(2):
+                for h in range(HALVES):
+                    nc.tensor.transpose(
+                        e_bank[c][:, i, h].rearrange("p u m -> p (u m)"),
+                        e_win[0][:].bitcast(F32)[:, :P],
+                        ident_f32[:],
+                    )
 
         w_grouped = const.tile([P, CH, PACK], BF16, align_bytes=64)
         for g in range(TILES):
-            w_t = psum.tile([P, PACK, P], BF16, tag="tr")
+            w_t = psum.tile([P, PACK, P], BF16, tag="tr", bufs=1)
             for t in range(PACK):
                 nc.tensor.transpose(w_t[:, t, :], w_rows[:, g, tile_cols(t)], ident_bf[:])
             nc.vector.tensor_copy(
@@ -131,10 +145,11 @@ def tile_mvpam_module_mask_cascade_pa_t_kernel(tc, x, q, k, mask0, wv0, bv0, out
 
         def group_x(b):
             x_grouped = work.tile([P, POS, PACK], BF16, align_bytes=64)
-            nc.scalar.copy(
-                out=x_grouped[:].rearrange("p (c i) t -> p c t i", i=4),
-                in_=live["x_rows", b][:].rearrange("p t (c i) -> p c t i", i=4),
-            )
+            for e in range(2):
+                nc.scalar.copy(
+                    out=x_grouped[:, e * 256 : (e + 1) * 256, :].rearrange("p (c i) t -> p c t i", i=4),
+                    in_=live["x_rows", b][:].rearrange("p t (c i e) -> p e c t i", i=4, e=2)[:, e],
+                )
             live["x_grouped", b] = x_grouped
 
         def quantise_x(b):
@@ -143,46 +158,48 @@ def tile_mvpam_module_mask_cascade_pa_t_kernel(tc, x, q, k, mask0, wv0, bv0, out
 
         def transpose_q(b):
             q_rows = live["q_rows", b]
-            q_t = psum.tile([P, TILES, P], BF16, tag="tr")
+            q_t = psum.tile([P, POS], BF16, tag="tr", bufs=1)
             for i in range(TILES):
-                nc.tensor.transpose(q_t[:, i, :], q_rows[:, i, :], ident_bf[:])
-            q_cols = work.tile([P, POS], BF16)
-            nc.scalar.copy(out=q_cols[:], in_=q_t[:].rearrange("p i m -> p (i m)"))
-            live["q_cols", b] = q_cols
+                nc.tensor.transpose(q_t[:, tile_cols(i)], q_rows[:, i, :], ident_bf[:])
+            nc.scalar.copy(
+                out=q_wide[b % 2][:, :, 0:3:2, :],
+                in_=q_t[:].rearrange("p (h i m) -> p i h m", h=HALVES, i=TILES),
+            )
 
         def softmax_numerator(b):
-            q_cols, k_rows = live["q_cols", b], live["k_rows", b]
+            k_rows = live["k_rows", b]
             neg_max = work.tile([P, TILES], F32)
             row_sum = work.tile([P, TILES], F32)
-            for pair in range(TILES // 2):
-                s_acc = psum.tile([P, 2, WINDOW], F32, tag="s")
-                for h in range(2):
-                    i = 2 * pair + h
-                    start_key = i * P - BAND
+            s_acc = psum.tile([P, TILES, WINDOW], F32, tag="s", bufs=1)
+            nc.tensor.matmul(
+                s_acc[:].rearrange("p i n -> p (i n)"),
+                lhsT=ident_bf[:],
+                rhs=mask_win[:].rearrange("p i n -> p (i n)"),
+                start=True,
+                stop=False,
+            )
+            for i in range(TILES):
+                q_tile = q_wide[b % 2][:, i].rearrange("p a m -> p (a m)")
+                for h in range(HALVES):
+                    start_key = (i + TILES * h) * GROUP - BAND
                     first, end = max(start_key, 0), min(start_key + WINDOW, POS)
                     nc.tensor.matmul(
-                        s_acc[:, h, :], lhsT=ident_bf[:], rhs=mask_win[:, i, :], start=True, stop=False
-                    )
-                    nc.tensor.matmul(
-                        s_acc[:, h, first - start_key : end - start_key],
-                        lhsT=q_cols[:, tile_cols(i)],
+                        s_acc[:, i, first - start_key : end - start_key],
+                        lhsT=q_tile[:, h * GROUP : h * GROUP + P],
                         rhs=k_rows[:, first:end],
                         start=False,
-                        stop=True,
+                        stop=(i == TILES - 1 and h == HALVES - 1),
                     )
-                nc.vector.tensor_reduce(
-                    out=neg_max[:, 2 * pair : 2 * pair + 2], in_=s_acc[:], axis=AXIS.X, op=ALU.max, negate=True
+            nc.vector.tensor_reduce(out=neg_max[:], in_=s_acc[:], axis=AXIS.X, op=ALU.max, negate=True)
+            for i in range(TILES):
+                nc.scalar.activation(
+                    out=e_win[b % 2][:, 2 * window_word(i) : 2 * (window_word(i) + PAIRS)],
+                    in_=s_acc[:, i, :],
+                    func=ACT.Exp,
+                    bias=neg_max[:, i : i + 1],
+                    scale=1.0,
+                    accum_out=row_sum[:, i : i + 1],
                 )
-                for h in range(2):
-                    i = 2 * pair + h
-                    nc.scalar.activation(
-                        out=e_win[b % 2][:, i, MARGIN : MARGIN + WINDOW],
-                        in_=s_acc[:, h, :],
-                        func=ACT.Exp,
-                        bias=neg_max[:, i : i + 1],
-                        scale=1.0,
-                        accum_out=row_sum[:, i : i + 1],
-                    )
             live["row_sum", b] = row_sum
 
         def values(b):
@@ -190,8 +207,9 @@ def tile_mvpam_module_mask_cascade_pa_t_kernel(tc, x, q, k, mask0, wv0, bv0, out
             v_grouped = work.tile([P, CH, PACK], BF16, align_bytes=64)
             for g in range(TILES):
                 v_acc = psum.tile([P, PACK, P], F32, tag="acc", bufs=4)
-                for t in range(PACK):
-                    mx_pass(nc, v_acc[:, t, :], x_mx, tile_cols(t), w_mx, tile_cols(g))
+                for u in range(2):
+                    for e in range(2):
+                        mx_pass(nc, v_acc[:, 2 * u + e, :], x_mx, tile_cols(2 * e + u), w_mx, tile_cols(g))
                 nc.vector.tensor_tensor(
                     out=v_grouped[:, tile_cols(g), :],
                     in0=v_acc[:].rearrange("p t c -> p c t"),
@@ -205,22 +223,30 @@ def tile_mvpam_module_mask_cascade_pa_t_kernel(tc, x, q, k, mask0, wv0, bv0, out
             quantise(nc, live["v_grouped", b], live["v_mx", b])
 
         def transpose_e(b):
-            e_t = psum.tile([P, TILES, 2, P], BF16, tag="tr")
-            planes = [sorted(((i, 0), ((i + 1) % TILES, 1))) for i in range(TILES)]
+            words = e_win[b % 2][:].bitcast(F32)
             for i in range(TILES):
-                for u in range(2):
-                    half = planes[i][u][1]
-                    nc.tensor.transpose(e_t[:, i, u, :], e_win[b % 2][:, i, tile_cols(half)], ident_bf[:])
-            for i in range(TILES):
-                low, high = planes[i][0][0], planes[i][1][0]
+                at = 32 * i - 16
+                blocks = e_bank[i // 2][:, i % 2].rearrange("p h u m -> p (h u) m")
+                places = [(at, slice(0, 4, 3))]
+                if at < 0:
+                    places.append((at + P, slice(1, 3)))
+                if at + PAIRS > P:
+                    places.append((at - P, slice(1, 3)))
+                for place, hu in places:
+                    begin = window_word(i) - place
+                    nc.tensor.transpose(blocks[:, hu, :], words[:, begin : begin + P], ident_f32[:])
+            e_grouped = work.tile([P, POS, PACK], BF16, align_bytes=64)
+            e_words = e_grouped[:].rearrange("p m j -> p (m j)").bitcast(F32)
+            for c in range(2):
                 nc.scalar.copy(
-                    out=e_grouped[b % 2][:, tile_cols(i), low : high + 1 : high - low],
-                    in_=e_t[:, i, :, :].rearrange("p u m -> p m u"),
+                    out=e_words[:, c * POS : (c + 1) * POS].rearrange("p (a m u) -> p a m u", m=GROUP, u=2),
+                    in_=e_bank[c][:].rearrange("p i h u m -> p (i h) m u"),
                 )
+            live["e_grouped", b] = e_grouped
 
         def quantise_e(b):
             live["e_mx", b] = mx_operand(work, POS, "e")
-            quantise(nc, e_grouped[b % 2], live["e_mx", b])
+            quantise(nc, live["e_grouped", b], live["e_mx", b])
 
         def reciprocal_sums(b):
             recip = work.tile([P, TILES], F32)
@@ -229,7 +255,7 @@ def tile_mvpam_module_mask_cascade_pa_t_kernel(tc, x, q, k, mask0, wv0, bv0, out
 
         def spread_reciprocals(b):
             recip = live["recip", b]
-            r_t = psum.tile([P, POS], F32, tag="tr")
+            r_t = psum.tile([P, POS], F32, tag="acc", bufs=4)
             for i in range(TILES):
                 nc.tensor.transpose(r_t[:, tile_cols(i)], recip[:, i : i + 1].to_broadcast([P, P]), ident_f32[:])
             recip_all = work.tile([P, POS], F32)
@@ -242,7 +268,12 @@ def tile_mvpam_module_mask_cascade_pa_t_kernel(tc, x, q, k, mask0, wv0, bv0, out
                 o_acc = psum.tile([P, POS], F32, tag="acc", bufs=4)
                 mx_pass(nc, o_acc[:], v_mx, tile_cols(g), e_mx, slice(0, POS))
                 o_rows = store.tile([P, POS], F32)
-                nc.vector.tensor_tensor(out=o_rows[:], in0=o_acc[:], in1=recip_all[:], op=ALU.mult)
+                nc.vector.tensor_tensor(
+                    out=o_rows[:].rearrange("p (h i m) -> p i h m", h=HALVES, i=TILES),
+                    in0=o_acc[:].rearrange("p (i h m) -> p i h m", h=HALVES, i=TILES),
+                    in1=recip_all[:].rearrange("p (i h m) -> p i h m", h=HALVES, i=TILES),
+                    op=ALU.mult,
+                )
                 nc.sync.dma_start(out=out[b, tile_cols(g), :], in_=o_rows[:])
 
         for j in range(BATCH + 2):

@@ -24,6 +24,7 @@ HALVES = 2
 PAIRS = WINDOW // 2
 MARGIN = P - 16
 E_WORDS = MARGIN + TILES * (PAIRS + MARGIN)
+GPSIMD_TILE = 3
 
 FLOPS = BATCH * (2 * CH * CH * POS + 2 * POS * HEAD * POS + 2 * CH * POS * POS)
 
@@ -142,6 +143,11 @@ def tile_mvpam_module_mask_cascade_pa_t_kernel(tc, x, q, k, mask0, wv0, bv0, out
             )
         w_mx = mx_operand(const, CH, "w")
         quantise(nc, w_grouped, w_mx)
+        bias_words = const.tile([P, P, PACK], F32)
+        nc.vector.tensor_copy(
+            out=bias_words[:],
+            in_=bias_all[:, tile_cols(GPSIMD_TILE)].unsqueeze(2).to_broadcast([P, P, PACK]),
+        )
 
         def group_x(b):
             x_grouped = work.tile([P, POS, PACK], BF16, align_bytes=64)
@@ -205,11 +211,18 @@ def tile_mvpam_module_mask_cascade_pa_t_kernel(tc, x, q, k, mask0, wv0, bv0, out
         def values(b):
             x_mx = live["x_mx", b]
             v_grouped = work.tile([P, CH, PACK], BF16, align_bytes=64)
-            for g in range(TILES):
+            for g in (GPSIMD_TILE,) + tuple(g for g in range(TILES) if g != GPSIMD_TILE):
                 v_acc = psum.tile([P, PACK, P], F32, tag="acc", bufs=4)
                 for u in range(2):
                     for e in range(2):
                         mx_pass(nc, v_acc[:, 2 * u + e, :], x_mx, tile_cols(2 * e + u), w_mx, tile_cols(g))
+                if g == GPSIMD_TILE:
+                    v_rows = work.tile([P, P, PACK], F32)
+                    nc.scalar.copy(out=v_rows[:], in_=v_acc[:].rearrange("p t c -> p c t"))
+                    nc.gpsimd.tensor_tensor(
+                        out=v_grouped[:, tile_cols(g), :], in0=v_rows[:], in1=bias_words[:], op=ALU.add
+                    )
+                    continue
                 nc.vector.tensor_tensor(
                     out=v_grouped[:, tile_cols(g), :],
                     in0=v_acc[:].rearrange("p t c -> p c t"),

@@ -25,6 +25,7 @@ PAIRS = WINDOW // 2
 MARGIN = P - 16
 E_WORDS = MARGIN + TILES * (PAIRS + MARGIN)
 GPSIMD_TILE = 3
+GPSIMD_FIRST = (GPSIMD_TILE,) + tuple(g for g in range(TILES) if g != GPSIMD_TILE)
 
 FLOPS = BATCH * (2 * CH * CH * POS + 2 * POS * HEAD * POS + 2 * CH * POS * POS)
 
@@ -211,7 +212,7 @@ def tile_mvpam_module_mask_cascade_pa_t_kernel(tc, x, q, k, mask0, wv0, bv0, out
         def values(b):
             x_mx = live["x_mx", b]
             v_grouped = work.tile([P, CH, PACK], BF16, align_bytes=64)
-            for g in (GPSIMD_TILE,) + tuple(g for g in range(TILES) if g != GPSIMD_TILE):
+            for g in GPSIMD_FIRST:
                 v_acc = psum.tile([P, PACK, P], F32, tag="acc", bufs=4)
                 for u in range(2):
                     for e in range(2):
@@ -277,13 +278,19 @@ def tile_mvpam_module_mask_cascade_pa_t_kernel(tc, x, q, k, mask0, wv0, bv0, out
 
         def result(b):
             v_mx, e_mx, recip_all = live["v_mx", b], live["e_mx", b], live["recip_all", b]
-            for g in range(TILES):
+            for g in GPSIMD_FIRST:
                 o_acc = psum.tile([P, POS], F32, tag="acc", bufs=4)
                 mx_pass(nc, o_acc[:], v_mx, tile_cols(g), e_mx, slice(0, POS))
                 o_rows = store.tile([P, POS], F32)
-                nc.vector.tensor_tensor(
+                if g == GPSIMD_TILE:
+                    o_raw = work.tile([P, POS], F32)
+                    nc.scalar.copy(out=o_raw[:], in_=o_acc[:])
+                    multiply, sums = nc.gpsimd.tensor_tensor, o_raw
+                else:
+                    multiply, sums = nc.vector.tensor_tensor, o_acc
+                multiply(
                     out=o_rows[:].rearrange("p (h i m) -> p i h m", h=HALVES, i=TILES),
-                    in0=o_acc[:].rearrange("p (i h m) -> p i h m", h=HALVES, i=TILES),
+                    in0=sums[:].rearrange("p (i h m) -> p i h m", h=HALVES, i=TILES),
                     in1=recip_all[:].rearrange("p (i h m) -> p i h m", h=HALVES, i=TILES),
                     op=ALU.mult,
                 )

@@ -81,7 +81,7 @@ def tile_mvpam_module_mask_cascade_pa_t_kernel(tc, x, q, k, mask0, wv0, bv0, out
     with ExitStack() as ctx:
         ctx.enter_context(tc.manual_schedule())
         const = ctx.enter_context(tc.tile_pool(name="const", bufs=1))
-        load = ctx.enter_context(tc.tile_pool(name="load", bufs=3))
+        load = ctx.enter_context(tc.tile_pool(name="load", bufs=4))
         work = ctx.enter_context(tc.tile_pool(name="work", bufs=2))
         store = ctx.enter_context(tc.tile_pool(name="store", bufs=6))
         psum = ctx.enter_context(tc.psum_pool(name="psum", bufs=2))
@@ -152,12 +152,21 @@ def tile_mvpam_module_mask_cascade_pa_t_kernel(tc, x, q, k, mask0, wv0, bv0, out
 
         def group_x(b):
             x_grouped = work.tile([P, POS, PACK], BF16, align_bytes=64)
-            for e in range(2):
-                nc.scalar.copy(
-                    out=x_grouped[:, e * 256 : (e + 1) * 256, :].rearrange("p (c i) t -> p c t i", i=4),
-                    in_=live["x_rows", b][:].rearrange("p t (c i e) -> p e c t i", i=4, e=2)[:, e],
-                )
+            nc.scalar.copy(
+                out=x_grouped[:, 0 : POS // 2, :].rearrange("p (c i) t -> p c t i", i=4),
+                in_=live["x_rows", b][:].rearrange("p t (c i e) -> p e c t i", i=4, e=2)[:, 0],
+            )
             live["x_grouped", b] = x_grouped
+
+        def group_odd_x(b):
+            nc.gpsimd.tensor_scalar(
+                out=live["x_grouped", b][:, POS // 2 : POS, :],
+                in0=live["x_rows", b][:].rearrange("p t (w e) -> p e w t", e=2)[:, 1],
+                scalar1=1.0,
+                scalar2=0.0,
+                op0=ALU.mult,
+                op1=ALU.add,
+            )
 
         def quantise_x(b):
             live["x_mx", b] = mx_operand(work, POS, "x")
@@ -168,15 +177,16 @@ def tile_mvpam_module_mask_cascade_pa_t_kernel(tc, x, q, k, mask0, wv0, bv0, out
             q_t = psum.tile([P, POS], BF16, tag="tr", bufs=1)
             for i in range(TILES):
                 nc.tensor.transpose(q_t[:, tile_cols(i)], q_rows[:, i, :], ident_bf[:])
+            live["q_t", b] = q_t
+
+        def widen_q(b):
             nc.scalar.copy(
                 out=q_wide[b % 2][:, :, 0:3:2, :],
-                in_=q_t[:].rearrange("p (h i m) -> p i h m", h=HALVES, i=TILES),
+                in_=live["q_t", b][:].rearrange("p (h i m) -> p i h m", h=HALVES, i=TILES),
             )
 
-        def softmax_numerator(b):
+        def scores(b):
             k_rows = live["k_rows", b]
-            neg_max = work.tile([P, TILES], F32)
-            row_sum = work.tile([P, TILES], F32)
             s_acc = psum.tile([P, TILES, WINDOW], F32, tag="s", bufs=1)
             nc.tensor.matmul(
                 s_acc[:].rearrange("p i n -> p (i n)"),
@@ -197,7 +207,13 @@ def tile_mvpam_module_mask_cascade_pa_t_kernel(tc, x, q, k, mask0, wv0, bv0, out
                         start=False,
                         stop=(i == TILES - 1 and h == HALVES - 1),
                     )
+            neg_max = work.tile([P, TILES], F32)
             nc.vector.tensor_reduce(out=neg_max[:], in_=s_acc[:], axis=AXIS.X, op=ALU.max, negate=True)
+            live["s_acc", b], live["neg_max", b] = s_acc, neg_max
+
+        def exponentials(b):
+            s_acc, neg_max = live["s_acc", b], live["neg_max", b]
+            row_sum = work.tile([P, TILES], F32)
             for i in range(TILES):
                 nc.scalar.activation(
                     out=e_win[b % 2][:, 2 * window_word(i) : 2 * (window_word(i) + PAIRS)],
@@ -249,6 +265,8 @@ def tile_mvpam_module_mask_cascade_pa_t_kernel(tc, x, q, k, mask0, wv0, bv0, out
                 for place, hu in places:
                     begin = window_word(i) - place
                     nc.tensor.transpose(blocks[:, hu, :], words[:, begin : begin + P], ident_f32[:])
+
+        def group_e(b):
             e_grouped = work.tile([P, POS, PACK], BF16, align_bytes=64)
             e_words = e_grouped[:].rearrange("p m j -> p (m j)").bitcast(F32)
             for c in range(2):
@@ -272,8 +290,11 @@ def tile_mvpam_module_mask_cascade_pa_t_kernel(tc, x, q, k, mask0, wv0, bv0, out
             r_t = psum.tile([P, POS], F32, tag="acc", bufs=4)
             for i in range(TILES):
                 nc.tensor.transpose(r_t[:, tile_cols(i)], recip[:, i : i + 1].to_broadcast([P, P]), ident_f32[:])
+            live["r_t", b] = r_t
+
+        def keep_reciprocals(b):
             recip_all = work.tile([P, POS], F32)
-            nc.scalar.copy(out=recip_all[:], in_=r_t[:])
+            nc.scalar.copy(out=recip_all[:], in_=live["r_t", b][:])
             live["recip_all", b] = recip_all
 
         def result(b):
@@ -296,26 +317,28 @@ def tile_mvpam_module_mask_cascade_pa_t_kernel(tc, x, q, k, mask0, wv0, bv0, out
                 )
                 nc.sync.dma_start(out=out[b, tile_cols(g), :], in_=o_rows[:])
 
-        for j in range(BATCH + 2):
-            front, middle, end_item = j, j - 1, j - 2
-            if front + 1 < BATCH:
-                load_inputs(front + 1)
-            if 0 <= middle < BATCH:
-                values(middle)
-                reciprocal_sums(middle)
-            if 0 <= end_item:
-                result(end_item)
-            if front < BATCH:
-                group_x(front)
-                quantise_x(front)
-            if 0 <= middle < BATCH:
-                quantise_values(middle)
-            if front < BATCH:
-                transpose_q(front)
-            if 0 <= middle < BATCH:
-                transpose_e(middle)
-                spread_reciprocals(middle)
-            if front < BATCH:
-                softmax_numerator(front)
-            if 0 <= middle < BATCH:
-                quantise_e(middle)
+        steps = (
+            (scores, 1),
+            (values, 1),
+            (group_x, 0),
+            (exponentials, 1),
+            (group_odd_x, 0),
+            (transpose_q, 0),
+            (result, 3),
+            (widen_q, 0),
+            (reciprocal_sums, 1),
+            (transpose_e, 1),
+            (spread_reciprocals, 2),
+            (group_e, 1),
+            (quantise_x, 0),
+            (keep_reciprocals, 2),
+            (quantise_values, 1),
+            (quantise_e, 1),
+        )
+        load_inputs(1)
+        for j in range(BATCH + 3):
+            if j + 2 < BATCH:
+                load_inputs(j + 2)
+            for step, lag in steps:
+                if 0 <= j - lag < BATCH:
+                    step(j - lag)

@@ -152,21 +152,12 @@ def tile_mvpam_module_mask_cascade_pa_t_kernel(tc, x, q, k, mask0, wv0, bv0, out
 
         def group_x(b):
             x_grouped = work.tile([P, POS, PACK], BF16, align_bytes=64)
-            nc.scalar.copy(
-                out=x_grouped[:, 0 : POS // 2, :].rearrange("p (c i) t -> p c t i", i=4),
-                in_=live["x_rows", b][:].rearrange("p t (c i e) -> p e c t i", i=4, e=2)[:, 0],
-            )
+            for e in range(2):
+                nc.scalar.copy(
+                    out=x_grouped[:, e * 256 : (e + 1) * 256, :].rearrange("p (c i) t -> p c t i", i=4),
+                    in_=live["x_rows", b][:].rearrange("p t (c i e) -> p e c t i", i=4, e=2)[:, e],
+                )
             live["x_grouped", b] = x_grouped
-
-        def group_odd_x(b):
-            nc.gpsimd.tensor_scalar(
-                out=live["x_grouped", b][:, POS // 2 : POS, :],
-                in0=live["x_rows", b][:].rearrange("p t (w e) -> p e w t", e=2)[:, 1],
-                scalar1=1.0,
-                scalar2=0.0,
-                op0=ALU.mult,
-                op1=ALU.add,
-            )
 
         def quantise_x(b):
             live["x_mx", b] = mx_operand(work, POS, "x")
@@ -318,25 +309,24 @@ def tile_mvpam_module_mask_cascade_pa_t_kernel(tc, x, q, k, mask0, wv0, bv0, out
                 nc.sync.dma_start(out=out[b, tile_cols(g), :], in_=o_rows[:])
 
         steps = (
-            (scores, 1),
-            (values, 1),
             (group_x, 0),
+            (scores, 1),
             (exponentials, 1),
-            (group_odd_x, 0),
             (transpose_q, 0),
-            (result, 3),
-            (widen_q, 0),
-            (reciprocal_sums, 1),
-            (transpose_e, 1),
-            (spread_reciprocals, 2),
-            (group_e, 1),
+            (quantise_values, 2),
             (quantise_x, 0),
+            (values, 1),
+            (transpose_e, 1),
+            (reciprocal_sums, 1),
             (keep_reciprocals, 2),
-            (quantise_values, 1),
+            (result, 2),
+            (widen_q, 0),
+            (group_e, 1),
             (quantise_e, 1),
+            (spread_reciprocals, 1),
         )
         load_inputs(1)
-        for j in range(BATCH + 3):
+        for j in range(BATCH + 2):
             if j + 2 < BATCH:
                 load_inputs(j + 2)
             for step, lag in steps:

@@ -24,8 +24,9 @@ HALVES = 2
 PAIRS = WINDOW // 2
 MARGIN = P - 16
 E_WORDS = MARGIN + TILES * (PAIRS + MARGIN)
-GPSIMD_TILE = 3
-GPSIMD_FIRST = (GPSIMD_TILE,) + tuple(g for g in range(TILES) if g != GPSIMD_TILE)
+SIDE_TILE = 3
+OTHER_TILES = tuple(g for g in range(TILES) if g != SIDE_TILE)
+SCALAR_X = 192
 
 FLOPS = BATCH * (2 * CH * CH * POS + 2 * POS * HEAD * POS + 2 * CH * POS * POS)
 
@@ -144,18 +145,25 @@ def tile_mvpam_module_mask_cascade_pa_t_kernel(tc, x, q, k, mask0, wv0, bv0, out
             )
         w_mx = mx_operand(const, CH, "w")
         quantise(nc, w_grouped, w_mx)
-        bias_words = const.tile([P, P, PACK], F32)
-        nc.vector.tensor_copy(
-            out=bias_words[:],
-            in_=bias_all[:, tile_cols(GPSIMD_TILE)].unsqueeze(2).to_broadcast([P, P, PACK]),
-        )
+        bias_t = psum.tile([P, P], BF16, tag="tr", bufs=1)
+        nc.tensor.transpose(bias_t[:], bias_all[:, tile_cols(SIDE_TILE)], ident_bf[:])
+        bias_col = const.tile([P, 1], F32)
+        nc.scalar.copy(out=bias_col[:], in_=bias_t[:, 0:1])
 
         def group_x(b):
-            x_grouped = work.tile([P, POS, PACK], BF16, align_bytes=64)
-            for e in range(2):
-                nc.scalar.copy(
-                    out=x_grouped[:, e * 256 : (e + 1) * 256, :].rearrange("p (c i) t -> p c t i", i=4),
-                    in_=live["x_rows", b][:].rearrange("p t (c i e) -> p e c t i", i=4, e=2)[:, e],
+            x_grouped = work.tile([P, POS, PACK], BF16, bufs=1, align_bytes=64)
+            nc.scalar.copy(
+                out=x_grouped[:, 0:SCALAR_X, :].rearrange("p (c i) t -> p c t i", i=4),
+                in_=live["x_rows", b][:].rearrange("p t (c i e) -> p e c t i", i=4, e=2)[:, 0, : SCALAR_X // 4],
+            )
+            for e, first in ((0, SCALAR_X), (1, 0)):
+                nc.gpsimd.tensor_scalar(
+                    out=x_grouped[:, e * 256 + first : (e + 1) * 256, :],
+                    in0=live["x_rows", b][:].rearrange("p t (w e) -> p e w t", e=2)[:, e, first:],
+                    scalar1=1.0,
+                    scalar2=0.0,
+                    op0=ALU.mult,
+                    op1=ALU.add,
                 )
             live["x_grouped", b] = x_grouped
 
@@ -198,9 +206,13 @@ def tile_mvpam_module_mask_cascade_pa_t_kernel(tc, x, q, k, mask0, wv0, bv0, out
                         start=False,
                         stop=(i == TILES - 1 and h == HALVES - 1),
                     )
+            live["s_acc", b] = s_acc
+
+        def maxima(b):
+            s_acc = live["s_acc", b]
             neg_max = work.tile([P, TILES], F32)
             nc.vector.tensor_reduce(out=neg_max[:], in_=s_acc[:], axis=AXIS.X, op=ALU.max, negate=True)
-            live["s_acc", b], live["neg_max", b] = s_acc, neg_max
+            live["neg_max", b] = neg_max
 
         def exponentials(b):
             s_acc, neg_max = live["s_acc", b], live["neg_max", b]
@@ -219,18 +231,16 @@ def tile_mvpam_module_mask_cascade_pa_t_kernel(tc, x, q, k, mask0, wv0, bv0, out
         def values(b):
             x_mx = live["x_mx", b]
             v_grouped = work.tile([P, CH, PACK], BF16, align_bytes=64)
-            for g in GPSIMD_FIRST:
+            v_acc = psum.tile([P, POS], F32, tag="acc", bufs=4)
+            mx_pass(nc, v_acc[:], w_mx, tile_cols(SIDE_TILE), x_mx, slice(0, POS))
+            v_cols = work.tile([P, POS], BF16)
+            nc.scalar.activation(out=v_cols[:], in_=v_acc[:], func=ACT.Identity, bias=bias_col[:], scale=1.0)
+            live["v_cols", b] = v_cols
+            for g in OTHER_TILES:
                 v_acc = psum.tile([P, PACK, P], F32, tag="acc", bufs=4)
                 for u in range(2):
                     for e in range(2):
                         mx_pass(nc, v_acc[:, 2 * u + e, :], x_mx, tile_cols(2 * e + u), w_mx, tile_cols(g))
-                if g == GPSIMD_TILE:
-                    v_rows = work.tile([P, P, PACK], F32)
-                    nc.scalar.copy(out=v_rows[:], in_=v_acc[:].rearrange("p t c -> p c t"))
-                    nc.gpsimd.tensor_tensor(
-                        out=v_grouped[:, tile_cols(g), :], in0=v_rows[:], in1=bias_words[:], op=ALU.add
-                    )
-                    continue
                 nc.vector.tensor_tensor(
                     out=v_grouped[:, tile_cols(g), :],
                     in0=v_acc[:].rearrange("p t c -> p c t"),
@@ -238,6 +248,16 @@ def tile_mvpam_module_mask_cascade_pa_t_kernel(tc, x, q, k, mask0, wv0, bv0, out
                     op=ALU.add,
                 )
             live["v_grouped", b] = v_grouped
+
+        def turn_values(b):
+            v_cols = live["v_cols", b]
+            v_t = psum.tile([P, PACK, P], BF16, tag="tr", bufs=1)
+            for u in range(2):
+                for e in range(2):
+                    nc.tensor.transpose(v_t[:, 2 * u + e, :], v_cols[:, tile_cols(2 * e + u)], ident_bf[:])
+            nc.scalar.copy(
+                out=live["v_grouped", b][:, tile_cols(SIDE_TILE), :], in_=v_t[:].rearrange("p t c -> p c t")
+            )
 
         def quantise_values(b):
             live["v_mx", b] = mx_operand(work, CH, "v")
@@ -290,11 +310,12 @@ def tile_mvpam_module_mask_cascade_pa_t_kernel(tc, x, q, k, mask0, wv0, bv0, out
 
         def result(b):
             v_mx, e_mx, recip_all = live["v_mx", b], live["e_mx", b], live["recip_all", b]
-            for g in GPSIMD_FIRST:
+            stores = []
+            for g in (SIDE_TILE,) + OTHER_TILES:
                 o_acc = psum.tile([P, POS], F32, tag="acc", bufs=4)
                 mx_pass(nc, o_acc[:], v_mx, tile_cols(g), e_mx, slice(0, POS))
                 o_rows = store.tile([P, POS], F32)
-                if g == GPSIMD_TILE:
+                if g == SIDE_TILE:
                     o_raw = work.tile([P, POS], F32)
                     nc.scalar.copy(out=o_raw[:], in_=o_acc[:])
                     multiply, sums = nc.gpsimd.tensor_tensor, o_raw
@@ -306,27 +327,31 @@ def tile_mvpam_module_mask_cascade_pa_t_kernel(tc, x, q, k, mask0, wv0, bv0, out
                     in1=recip_all[:].rearrange("p (i h m) -> p i h m", h=HALVES, i=TILES),
                     op=ALU.mult,
                 )
+                stores.append((g, o_rows))
+            for g, o_rows in stores[1:] + stores[:1]:
                 nc.sync.dma_start(out=out[b, tile_cols(g), :], in_=o_rows[:])
 
         steps = (
             (group_x, 0),
-            (scores, 1),
+            (maxima, 1),
             (exponentials, 1),
+            (values, 1),
             (transpose_q, 0),
+            (widen_q, 0),
+            (transpose_e, 1),
             (quantise_values, 2),
             (quantise_x, 0),
-            (values, 1),
-            (transpose_e, 1),
-            (reciprocal_sums, 1),
-            (keep_reciprocals, 2),
-            (result, 2),
-            (widen_q, 0),
+            (quantise_e, 2),
+            (result, 3),
+            (spread_reciprocals, 2),
             (group_e, 1),
-            (quantise_e, 1),
-            (spread_reciprocals, 1),
+            (turn_values, 1),
+            (keep_reciprocals, 2),
+            (scores, 0),
+            (reciprocal_sums, 1),
         )
         load_inputs(1)
-        for j in range(BATCH + 2):
+        for j in range(BATCH + 3):
             if j + 2 < BATCH:
                 load_inputs(j + 2)
             for step, lag in steps:

@@ -332,23 +332,23 @@ def tile_mvpam_module_mask_cascade_pa_t_kernel(tc, x, q, k, mask0, wv0, bv0, out
                 nc.sync.dma_start(out=out[b, tile_cols(g), :], in_=o_rows[:])
 
         steps = (
-            (group_x, 0),
-            (maxima, 1),
-            (exponentials, 1),
             (values, 1),
+            (exponentials, 1),
             (transpose_q, 0),
-            (widen_q, 0),
-            (transpose_e, 1),
-            (quantise_values, 2),
-            (quantise_x, 0),
             (quantise_e, 2),
-            (result, 3),
+            (group_x, 0),
+            (quantise_values, 2),
+            (widen_q, 0),
             (spread_reciprocals, 2),
+            (quantise_x, 0),
+            (transpose_e, 1),
+            (keep_reciprocals, 2),
+            (reciprocal_sums, 1),
+            (result, 3),
             (group_e, 1),
             (turn_values, 1),
-            (keep_reciprocals, 2),
             (scores, 0),
-            (reciprocal_sums, 1),
+            (maxima, 0),
         )
         load_inputs(1)
         for j in range(BATCH + 3):

@@ -89,30 +89,51 @@ def tile_mvpam_module_mask_cascade_pa_t_kernel(tc, x, q, k, mask0, wv0, bv0, out
 
         live = {}
 
-        def load_inputs(b):
+        def load_x(b):
             x_rows = load.tile([P, PACK, POS], BF16)
             nc.sync.dma_start(out=x_rows[:], in_=x[b].rearrange("(t p) n -> p t n", p=P))
+            live["x_rows", b] = x_rows
+
+        def load_heads(b):
             q_rows = load.tile([P, TILES, HEAD], BF16)
             nc.sync.dma_start(out=q_rows[:], in_=q[b].rearrange("(i p) d -> p i d", p=P))
             k_rows = load.tile([P, POS], BF16)
             nc.sync.dma_start(out=k_rows[:], in_=k[b])
-            live["x_rows", b], live["q_rows", b], live["k_rows", b] = x_rows, q_rows, k_rows
+            live["q_rows", b], live["k_rows", b] = q_rows, k_rows
 
+        load_x(0)
         w_rows = const.tile([P, TILES, CH], BF16)
-        nc.sync.dma_start(out=w_rows[:], in_=wv0.rearrange("(g p) k -> p g k", p=P))
-        load_inputs(0)
+        for g in range(TILES):
+            nc.sync.dma_start(out=w_rows[:, g, :], in_=wv0[tile_cols(g), :])
+        load_heads(0)
         mask_win = const.tile([P, TILES, WINDOW], BF16)
-        for i in range(TILES):
-            for h in range(HALVES):
-                g = i + TILES * h
-                for offset, first, end in cyclic_pieces(g * GROUP - BAND, WINDOW, POS):
-                    nc.scalar.dma_start(
-                        out=mask_win[h * GROUP : (h + 1) * GROUP, i, offset : offset + end - first],
-                        in_=mask0[g * GROUP : (g + 1) * GROUP, first:end],
-                    )
-        bias_all = const.tile([P, CH], BF16)
-        nc.scalar.dma_start(out=bias_all[:], in_=bv0.partition_broadcast(P))
+        diagonal = GROUP * POS + GROUP
+        for h, whole in ((0, slice(1, TILES)), (1, slice(0, TILES - 1))):
+            rows = slice(h * GROUP, (h + 1) * GROUP)
+            g = whole.start + TILES * h
+            start = g * GROUP * POS + g * GROUP - BAND
+            nc.sync.dma_start(
+                out=mask_win[rows, whole, :],
+                in_=mask0.rearrange("m n -> (m n)")[start : start + (TILES - 1) * diagonal]
+                .rearrange("(i r) -> i r", r=diagonal)[:, : GROUP * POS]
+                .rearrange("i (m n) -> m i n", n=POS)[:, :, :WINDOW],
+            )
+            i = (TILES - 1) * h
+            g = i + TILES * h
+            for offset, first, end in cyclic_pieces(g * GROUP - BAND, WINDOW, POS):
+                nc.sync.dma_start(
+                    out=mask_win[rows, i, offset : offset + end - first],
+                    in_=mask0[g * GROUP : (g + 1) * GROUP, first:end],
+                )
+        warm = const.tile([P, 1], F32)
+        nc.vector.memset(warm[:], 0.0)
+        nc.scalar.activation(out=warm[:], in_=warm[:], func=ACT.Exp)
 
+        bias_row = const.tile([P, CH], BF16)
+        nc.vector.memset(bias_row[:], 0.0)
+        nc.scalar.dma_start(out=bias_row[0:1, :], in_=bv0.rearrange("(o c) -> o c", o=1))
+        ones = const.tile([P, P], BF16)
+        nc.vector.memset(ones[:], 1.0)
         ident_bf = const.tile([P, P], BF16)
         make_identity(nc, ident_bf[:])
         ident_f32 = const.tile([P, P], F32)
@@ -135,21 +156,6 @@ def tile_mvpam_module_mask_cascade_pa_t_kernel(tc, x, q, k, mask0, wv0, bv0, out
                         ident_f32[:],
                     )
 
-        w_grouped = const.tile([P, CH, PACK], BF16, align_bytes=64)
-        for g in range(TILES):
-            w_t = psum.tile([P, PACK, P], BF16, tag="tr", bufs=1)
-            for t in range(PACK):
-                nc.tensor.transpose(w_t[:, t, :], w_rows[:, g, tile_cols(t)], ident_bf[:])
-            nc.vector.tensor_copy(
-                out=w_grouped[:, tile_cols(g), :], in_=w_t[:].rearrange("p t c -> p c t")
-            )
-        w_mx = mx_operand(const, CH, "w")
-        quantise(nc, w_grouped, w_mx)
-        bias_t = psum.tile([P, P], BF16, tag="tr", bufs=1)
-        nc.tensor.transpose(bias_t[:], bias_all[:, tile_cols(SIDE_TILE)], ident_bf[:])
-        bias_col = const.tile([P, 1], F32)
-        nc.scalar.copy(out=bias_col[:], in_=bias_t[:, 0:1])
-
         def group_x(b):
             x_grouped = work.tile([P, POS, PACK], BF16, bufs=1, align_bytes=64)
             nc.scalar.copy(
@@ -157,7 +163,8 @@ def tile_mvpam_module_mask_cascade_pa_t_kernel(tc, x, q, k, mask0, wv0, bv0, out
                 in_=live["x_rows", b][:].rearrange("p t (c i e) -> p e c t i", i=4, e=2)[:, 0, : SCALAR_X // 4],
             )
             for e, first in ((0, SCALAR_X), (1, 0)):
-                nc.gpsimd.tensor_scalar(
+                engine = nc.vector if b == 0 and e == 1 else nc.gpsimd
+                engine.tensor_scalar(
                     out=x_grouped[:, e * 256 + first : (e + 1) * 256, :],
                     in0=live["x_rows", b][:].rearrange("p t (w e) -> p e w t", e=2)[:, e, first:],
                     scalar1=1.0,
@@ -166,6 +173,25 @@ def tile_mvpam_module_mask_cascade_pa_t_kernel(tc, x, q, k, mask0, wv0, bv0, out
                     op1=ALU.add,
                 )
             live["x_grouped", b] = x_grouped
+
+        group_x(0)
+        w_grouped = const.tile([P, CH, PACK], BF16, align_bytes=64)
+        for g in range(TILES):
+            w_t = psum.tile([P, PACK, P], BF16, tag="acc", bufs=4)
+            for t in range(PACK):
+                nc.tensor.transpose(w_t[:, t, :], w_rows[:, g, tile_cols(t)], ident_bf[:])
+            copy = nc.vector.tensor_copy if g % 2 == 0 else nc.scalar.copy
+            copy(out=w_grouped[:, tile_cols(g), :], in_=w_t[:].rearrange("p t c -> p c t"))
+        w_mx = mx_operand(const, CH, "w")
+        quantise(nc, w_grouped, w_mx)
+        bias_t = psum.tile([P, CH], F32, tag="acc", bufs=4)
+        nc.tensor.matmul(bias_t[:], lhsT=ones[:], rhs=bias_row[:], start=True, stop=True)
+        bias_all = const.tile([P, CH], BF16)
+        nc.scalar.copy(out=bias_all[:], in_=bias_t[:])
+        side_t = psum.tile([P, P], BF16, tag="tr", bufs=1)
+        nc.tensor.transpose(side_t[:], bias_row[:, tile_cols(SIDE_TILE)], ident_bf[:])
+        bias_col = const.tile([P, 1], F32)
+        nc.scalar.copy(out=bias_col[:], in_=side_t[:, 0:1])
 
         def quantise_x(b):
             live["x_mx", b] = mx_operand(work, POS, "x")
@@ -230,7 +256,8 @@ def tile_mvpam_module_mask_cascade_pa_t_kernel(tc, x, q, k, mask0, wv0, bv0, out
 
         def values(b):
             x_mx = live["x_mx", b]
-            v_grouped = work.tile([P, CH, PACK], BF16, align_bytes=64)
+            last_grouped = work.tile([P, CH + POS, PACK], BF16, align_bytes=64)
+            v_grouped = last_grouped[:, 0:CH, :]
             v_acc = psum.tile([P, POS], F32, tag="acc", bufs=4)
             mx_pass(nc, v_acc[:], w_mx, tile_cols(SIDE_TILE), x_mx, slice(0, POS))
             v_cols = work.tile([P, POS], BF16)
@@ -247,7 +274,7 @@ def tile_mvpam_module_mask_cascade_pa_t_kernel(tc, x, q, k, mask0, wv0, bv0, out
                     in1=bias_all[:, tile_cols(g)].unsqueeze(2).to_broadcast([P, P, PACK]),
                     op=ALU.add,
                 )
-            live["v_grouped", b] = v_grouped
+            live["last_grouped", b] = last_grouped
 
         def turn_values(b):
             v_cols = live["v_cols", b]
@@ -256,12 +283,12 @@ def tile_mvpam_module_mask_cascade_pa_t_kernel(tc, x, q, k, mask0, wv0, bv0, out
                 for e in range(2):
                     nc.tensor.transpose(v_t[:, 2 * u + e, :], v_cols[:, tile_cols(2 * e + u)], ident_bf[:])
             nc.scalar.copy(
-                out=live["v_grouped", b][:, tile_cols(SIDE_TILE), :], in_=v_t[:].rearrange("p t c -> p c t")
+                out=live["last_grouped", b][:, tile_cols(SIDE_TILE), :], in_=v_t[:].rearrange("p t c -> p c t")
             )
 
-        def quantise_values(b):
-            live["v_mx", b] = mx_operand(work, CH, "v")
-            quantise(nc, live["v_grouped", b], live["v_mx", b])
+        def quantise_last(b):
+            live["last_mx", b] = mx_operand(work, CH + POS, "last")
+            quantise(nc, live["last_grouped", b], live["last_mx", b])
 
         def transpose_e(b):
             words = e_win[b % 2][:].bitcast(F32)
@@ -278,19 +305,13 @@ def tile_mvpam_module_mask_cascade_pa_t_kernel(tc, x, q, k, mask0, wv0, bv0, out
                     nc.tensor.transpose(blocks[:, hu, :], words[:, begin : begin + P], ident_f32[:])
 
         def group_e(b):
-            e_grouped = work.tile([P, POS, PACK], BF16, align_bytes=64)
-            e_words = e_grouped[:].rearrange("p m j -> p (m j)").bitcast(F32)
+            e_grouped = live["last_grouped", b][:, CH : CH + POS, :]
+            e_words = e_grouped.rearrange("p m j -> p (m j)").bitcast(F32)
             for c in range(2):
                 nc.scalar.copy(
                     out=e_words[:, c * POS : (c + 1) * POS].rearrange("p (a m u) -> p a m u", m=GROUP, u=2),
                     in_=e_bank[c][:].rearrange("p i h u m -> p (i h) m u"),
                 )
-            live["e_grouped", b] = e_grouped
-
-        def quantise_e(b):
-            live["e_mx", b] = mx_operand(work, POS, "e")
-            quantise(nc, live["e_grouped", b], live["e_mx", b])
-
         def reciprocal_sums(b):
             recip = work.tile([P, TILES], F32)
             nc.vector.reciprocal(out=recip[:], in_=live["row_sum", b][:])
@@ -309,11 +330,11 @@ def tile_mvpam_module_mask_cascade_pa_t_kernel(tc, x, q, k, mask0, wv0, bv0, out
             live["recip_all", b] = recip_all
 
         def result(b):
-            v_mx, e_mx, recip_all = live["v_mx", b], live["e_mx", b], live["recip_all", b]
+            last_mx, recip_all = live["last_mx", b], live["recip_all", b]
             stores = []
             for g in (SIDE_TILE,) + OTHER_TILES:
                 o_acc = psum.tile([P, POS], F32, tag="acc", bufs=4)
-                mx_pass(nc, o_acc[:], v_mx, tile_cols(g), e_mx, slice(0, POS))
+                mx_pass(nc, o_acc[:], last_mx, tile_cols(g), last_mx, slice(CH, CH + POS))
                 o_rows = store.tile([P, POS], F32)
                 if g == SIDE_TILE:
                     o_raw = work.tile([P, POS], F32)
@@ -335,9 +356,8 @@ def tile_mvpam_module_mask_cascade_pa_t_kernel(tc, x, q, k, mask0, wv0, bv0, out
             (values, 1),
             (exponentials, 1),
             (transpose_q, 0),
-            (quantise_e, 2),
+            (quantise_last, 2),
             (group_x, 0),
-            (quantise_values, 2),
             (widen_q, 0),
             (spread_reciprocals, 2),
             (quantise_x, 0),
@@ -350,10 +370,12 @@ def tile_mvpam_module_mask_cascade_pa_t_kernel(tc, x, q, k, mask0, wv0, bv0, out
             (scores, 0),
             (maxima, 0),
         )
-        load_inputs(1)
+        load_x(1)
+        load_heads(1)
         for j in range(BATCH + 3):
             if j + 2 < BATCH:
-                load_inputs(j + 2)
+                load_x(j + 2)
+                load_heads(j + 2)
             for step, lag in steps:
-                if 0 <= j - lag < BATCH:
+                if 0 <= j - lag < BATCH and (step, j) != (group_x, 0):
                     step(j - lag)

from contextlib import ExitStack

import concourse.mybir as mybir
from concourse.masks import make_identity

BF16 = mybir.dt.bfloat16
F32 = mybir.dt.float32
U32 = mybir.dt.uint32
U8 = mybir.dt.uint8
FP8X4 = mybir.dt.float8_e4m3fn_x4
ACT = mybir.ActivationFunctionType
ALU = mybir.AluOpType
AXIS = mybir.AxisListType

P = 128
PACK = 4
BATCH, CH, HEAD, POS = 16, 512, 128, 512
TILES = POS // P
BAND = 32

GROUP = 64
WINDOW = GROUP + 2 * BAND
HALVES = 2
PAIRS = WINDOW // 2
MARGIN = P - 16
E_WORDS = MARGIN + TILES * (PAIRS + MARGIN)
SIDE_TILE = 3
OTHER_TILES = tuple(g for g in range(TILES) if g != SIDE_TILE)
SCALAR_X = 192

FLOPS = BATCH * (2 * CH * CH * POS + 2 * POS * HEAD * POS + 2 * CH * POS * POS)


def cyclic_pieces(start, width, period):
    pieces = []
    offset = 0
    while offset < width:
        first = (start + offset) % period
        length = min(width - offset, period - first)
        pieces.append((offset, first, first + length))
        offset += length
    return pieces


def quantise(nc, grouped, operand):
    codes, scales = operand
    nc.vector.quantize_mx(
        out=codes[:].bitcast(FP8X4),
        scales=scales[:],
        in_=grouped[:].rearrange("p w j -> p (w j)"),
    )


def mx_operand(pool, width, name):
    codes = pool.tile([P, width], U32, name=name + "_codes", align_bytes=64)
    scales = pool.tile([P, width], U8, name=name + "_scales", align_bytes=64)
    return codes, scales


def mx_pass(nc, acc, stationary, stationary_cols, moving, moving_cols):
    nc.tensor.matmul_mx(
        out=acc,
        lhsT=stationary[0][:, stationary_cols].bitcast(FP8X4),
        lhsT_scale=stationary[1][:, stationary_cols],
        rhs=moving[0][:, moving_cols].bitcast(FP8X4),
        rhs_scale=moving[1][:, moving_cols],
        start=True,
        stop=True,
    )


def tile_cols(i):
    return slice(i * P, (i + 1) * P)


def window_word(i):
    return MARGIN + i * (PAIRS + MARGIN)


def tile_mvpam_module_mask_cascade_pa_t_kernel(tc, x, q, k, mask0, wv0, bv0, out):
    nc = tc.nc
    with ExitStack() as ctx:
        ctx.enter_context(tc.manual_schedule())
        const = ctx.enter_context(tc.tile_pool(name="const", bufs=1))
        load = ctx.enter_context(tc.tile_pool(name="load", bufs=4))
        work = ctx.enter_context(tc.tile_pool(name="work", bufs=2))
        store = ctx.enter_context(tc.tile_pool(name="store", bufs=6))
        psum = ctx.enter_context(tc.psum_pool(name="psum", bufs=2))

        live = {}

        def load_x(b):
            x_rows = load.tile([P, PACK, POS], BF16)
            nc.sync.dma_start(out=x_rows[:], in_=x[b].rearrange("(t p) n -> p t n", p=P))
            live["x_rows", b] = x_rows

        def load_heads(b):
            q_rows = load.tile([P, TILES, HEAD], BF16)
            nc.sync.dma_start(out=q_rows[:], in_=q[b].rearrange("(i p) d -> p i d", p=P))
            k_rows = load.tile([P, POS], BF16)
            nc.sync.dma_start(out=k_rows[:], in_=k[b])
            live["q_rows", b], live["k_rows", b] = q_rows, k_rows

        load_x(0)
        w_rows = const.tile([P, TILES, CH], BF16)
        for g in range(TILES):
            nc.sync.dma_start(out=w_rows[:, g, :], in_=wv0[tile_cols(g), :])
        load_heads(0)
        mask_win = const.tile([P, TILES, WINDOW], BF16)
        diagonal = GROUP * POS + GROUP
        for h, whole in ((0, slice(1, TILES)), (1, slice(0, TILES - 1))):
            rows = slice(h * GROUP, (h + 1) * GROUP)
            g = whole.start + TILES * h
            start = g * GROUP * POS + g * GROUP - BAND
            nc.sync.dma_start(
                out=mask_win[rows, whole, :],
                in_=mask0.rearrange("m n -> (m n)")[start : start + (TILES - 1) * diagonal]
                .rearrange("(i r) -> i r", r=diagonal)[:, : GROUP * POS]
                .rearrange("i (m n) -> m i n", n=POS)[:, :, :WINDOW],
            )
            i = (TILES - 1) * h
            g = i + TILES * h
            for offset, first, end in cyclic_pieces(g * GROUP - BAND, WINDOW, POS):
                nc.sync.dma_start(
                    out=mask_win[rows, i, offset : offset + end - first],
                    in_=mask0[g * GROUP : (g + 1) * GROUP, first:end],
                )
        warm = const.tile([P, 1], F32)
        nc.vector.memset(warm[:], 0.0)
        nc.scalar.activation(out=warm[:], in_=warm[:], func=ACT.Exp)

        bias_row = const.tile([P, CH], BF16)
        nc.vector.memset(bias_row[:], 0.0)
        nc.scalar.dma_start(out=bias_row[0:1, :], in_=bv0.rearrange("(o c) -> o c", o=1))
        ones = const.tile([P, P], BF16)
        nc.vector.memset(ones[:], 1.0)
        ident_bf = const.tile([P, P], BF16)
        make_identity(nc, ident_bf[:])
        ident_f32 = const.tile([P, P], F32)
        make_identity(nc, ident_f32[:])

        e_win = [const.tile([P, 2 * E_WORDS], BF16, name="e_win%d" % h) for h in range(2)]
        q_wide = [const.tile([P, TILES, 3, GROUP], BF16, name="q_wide%d" % h) for h in range(2)]
        for h in range(2):
            nc.vector.memset(e_win[h][:], 0.0)
            nc.gpsimd.memset(q_wide[h][:], 0.0)
        e_bank = [
            psum.tile([P, 2, HALVES, 2, GROUP], F32, name="e_bank%d" % c, bufs=1) for c in range(2)
        ]
        for c in range(2):
            for i in range(2):
                for h in range(HALVES):
                    nc.tensor.transpose(
                        e_bank[c][:, i, h].rearrange("p u m -> p (u m)"),
                        e_win[0][:].bitcast(F32)[:, :P],
                        ident_f32[:],
                    )

        def group_x(b):
            x_grouped = work.tile([P, POS, PACK], BF16, bufs=1, align_bytes=64)
            nc.scalar.copy(
                out=x_grouped[:, 0:SCALAR_X, :].rearrange("p (c i) t -> p c t i", i=4),
                in_=live["x_rows", b][:].rearrange("p t (c i e) -> p e c t i", i=4, e=2)[:, 0, : SCALAR_X // 4],
            )
            for e, first in ((0, SCALAR_X), (1, 0)):
                engine = nc.vector if b == 0 and e == 1 else nc.gpsimd
                engine.tensor_scalar(
                    out=x_grouped[:, e * 256 + first : (e + 1) * 256, :],
                    in0=live["x_rows", b][:].rearrange("p t (w e) -> p e w t", e=2)[:, e, first:],
                    scalar1=1.0,
                    scalar2=0.0,
                    op0=ALU.mult,
                    op1=ALU.add,
                )
            live["x_grouped", b] = x_grouped

        group_x(0)
        w_grouped = const.tile([P, CH, PACK], BF16, align_bytes=64)
        for g in range(TILES):
            w_t = psum.tile([P, PACK, P], BF16, tag="acc", bufs=4)
            for t in range(PACK):
                nc.tensor.transpose(w_t[:, t, :], w_rows[:, g, tile_cols(t)], ident_bf[:])
            copy = nc.vector.tensor_copy if g % 2 == 0 else nc.scalar.copy
            copy(out=w_grouped[:, tile_cols(g), :], in_=w_t[:].rearrange("p t c -> p c t"))
        w_mx = mx_operand(const, CH, "w")
        quantise(nc, w_grouped, w_mx)
        bias_t = psum.tile([P, CH], F32, tag="acc", bufs=4)
        nc.tensor.matmul(bias_t[:], lhsT=ones[:], rhs=bias_row[:], start=True, stop=True)
        bias_all = const.tile([P, CH], BF16)
        nc.scalar.copy(out=bias_all[:], in_=bias_t[:])
        side_t = psum.tile([P, P], BF16, tag="tr", bufs=1)
        nc.tensor.transpose(side_t[:], bias_row[:, tile_cols(SIDE_TILE)], ident_bf[:])
        bias_col = const.tile([P, 1], F32)
        nc.scalar.copy(out=bias_col[:], in_=side_t[:, 0:1])

        def quantise_x(b):
            live["x_mx", b] = mx_operand(work, POS, "x")
            quantise(nc, live["x_grouped", b], live["x_mx", b])

        def transpose_q(b):
            q_rows = live["q_rows", b]
            q_t = psum.tile([P, POS], BF16, tag="tr", bufs=1)
            for i in range(TILES):
                nc.tensor.transpose(q_t[:, tile_cols(i)], q_rows[:, i, :], ident_bf[:])
            live["q_t", b] = q_t

        def widen_q(b):
            nc.scalar.copy(
                out=q_wide[b % 2][:, :, 0:3:2, :],
                in_=live["q_t", b][:].rearrange("p (h i m) -> p i h m", h=HALVES, i=TILES),
            )

        def scores(b):
            k_rows = live["k_rows", b]
            s_acc = psum.tile([P, TILES, WINDOW], F32, tag="s", bufs=1)
            nc.tensor.matmul(
                s_acc[:].rearrange("p i n -> p (i n)"),
                lhsT=ident_bf[:],
                rhs=mask_win[:].rearrange("p i n -> p (i n)"),
                start=True,
                stop=False,
            )
            for i in range(TILES):
                q_tile = q_wide[b % 2][:, i].rearrange("p a m -> p (a m)")
                for h in range(HALVES):
                    start_key = (i + TILES * h) * GROUP - BAND
                    first, end = max(start_key, 0), min(start_key + WINDOW, POS)
                    nc.tensor.matmul(
                        s_acc[:, i, first - start_key : end - start_key],
                        lhsT=q_tile[:, h * GROUP : h * GROUP + P],
                        rhs=k_rows[:, first:end],
                        start=False,
                        stop=(i == TILES - 1 and h == HALVES - 1),
                    )
            live["s_acc", b] = s_acc

        def maxima(b):
            s_acc = live["s_acc", b]
            neg_max = work.tile([P, TILES], F32)
            nc.vector.tensor_reduce(out=neg_max[:], in_=s_acc[:], axis=AXIS.X, op=ALU.max, negate=True)
            live["neg_max", b] = neg_max

        def exponentials(b):
            s_acc, neg_max = live["s_acc", b], live["neg_max", b]
            row_sum = work.tile([P, TILES], F32)
            for i in range(TILES):
                nc.scalar.activation(
                    out=e_win[b % 2][:, 2 * window_word(i) : 2 * (window_word(i) + PAIRS)],
                    in_=s_acc[:, i, :],
                    func=ACT.Exp,
                    bias=neg_max[:, i : i + 1],
                    scale=1.0,
                    accum_out=row_sum[:, i : i + 1],
                )
            live["row_sum", b] = row_sum

        def values(b):
            x_mx = live["x_mx", b]
            last_grouped = work.tile([P, CH + POS, PACK], BF16, align_bytes=64)
            v_grouped = last_grouped[:, 0:CH, :]
            v_acc = psum.tile([P, POS], F32, tag="acc", bufs=4)
            mx_pass(nc, v_acc[:], w_mx, tile_cols(SIDE_TILE), x_mx, slice(0, POS))
            v_cols = work.tile([P, POS], BF16)
            nc.scalar.activation(out=v_cols[:], in_=v_acc[:], func=ACT.Identity, bias=bias_col[:], scale=1.0)
            live["v_cols", b] = v_cols
            for g in OTHER_TILES:
                v_acc = psum.tile([P, PACK, P], F32, tag="acc", bufs=4)
                for u in range(2):
                    for e in range(2):
                        mx_pass(nc, v_acc[:, 2 * u + e, :], x_mx, tile_cols(2 * e + u), w_mx, tile_cols(g))
                nc.vector.tensor_tensor(
                    out=v_grouped[:, tile_cols(g), :],
                    in0=v_acc[:].rearrange("p t c -> p c t"),
                    in1=bias_all[:, tile_cols(g)].unsqueeze(2).to_broadcast([P, P, PACK]),
                    op=ALU.add,
                )
            live["last_grouped", b] = last_grouped

        def turn_values(b):
            v_cols = live["v_cols", b]
            v_t = psum.tile([P, PACK, P], BF16, tag="tr", bufs=1)
            for u in range(2):
                for e in range(2):
                    nc.tensor.transpose(v_t[:, 2 * u + e, :], v_cols[:, tile_cols(2 * e + u)], ident_bf[:])
            nc.scalar.copy(
                out=live["last_grouped", b][:, tile_cols(SIDE_TILE), :], in_=v_t[:].rearrange("p t c -> p c t")
            )

        def quantise_last(b):
            live["last_mx", b] = mx_operand(work, CH + POS, "last")
            quantise(nc, live["last_grouped", b], live["last_mx", b])

        def transpose_e(b):
            words = e_win[b % 2][:].bitcast(F32)
            for i in range(TILES):
                at = 32 * i - 16
                blocks = e_bank[i // 2][:, i % 2].rearrange("p h u m -> p (h u) m")
                places = [(at, slice(0, 4, 3))]
                if at < 0:
                    places.append((at + P, slice(1, 3)))
                if at + PAIRS > P:
                    places.append((at - P, slice(1, 3)))
                for place, hu in places:
                    begin = window_word(i) - place
                    nc.tensor.transpose(blocks[:, hu, :], words[:, begin : begin + P], ident_f32[:])

        def group_e(b):
            e_grouped = live["last_grouped", b][:, CH : CH + POS, :]
            e_words = e_grouped.rearrange("p m j -> p (m j)").bitcast(F32)
            for c in range(2):
                nc.scalar.copy(
                    out=e_words[:, c * POS : (c + 1) * POS].rearrange("p (a m u) -> p a m u", m=GROUP, u=2),
                    in_=e_bank[c][:].rearrange("p i h u m -> p (i h) m u"),
                )
        def reciprocal_sums(b):
            recip = work.tile([P, TILES], F32)
            nc.vector.reciprocal(out=recip[:], in_=live["row_sum", b][:])
            live["recip", b] = recip

        def spread_reciprocals(b):
            recip = live["recip", b]
            r_t = psum.tile([P, POS], F32, tag="acc", bufs=4)
            for i in range(TILES):
                nc.tensor.transpose(r_t[:, tile_cols(i)], recip[:, i : i + 1].to_broadcast([P, P]), ident_f32[:])
            live["r_t", b] = r_t

        def keep_reciprocals(b):
            recip_all = work.tile([P, POS], F32)
            nc.scalar.copy(out=recip_all[:], in_=live["r_t", b][:])
            live["recip_all", b] = recip_all

        def result(b):
            last_mx, recip_all = live["last_mx", b], live["recip_all", b]
            stores = []
            for g in (SIDE_TILE,) + OTHER_TILES:
                o_acc = psum.tile([P, POS], F32, tag="acc", bufs=4)
                mx_pass(nc, o_acc[:], last_mx, tile_cols(g), last_mx, slice(CH, CH + POS))
                o_rows = store.tile([P, POS], F32)
                if g == SIDE_TILE:
                    o_raw = work.tile([P, POS], F32)
                    nc.scalar.copy(out=o_raw[:], in_=o_acc[:])
                    multiply, sums = nc.gpsimd.tensor_tensor, o_raw
                else:
                    multiply, sums = nc.vector.tensor_tensor, o_acc
                multiply(
                    out=o_rows[:].rearrange("p (h i m) -> p i h m", h=HALVES, i=TILES),
                    in0=sums[:].rearrange("p (i h m) -> p i h m", h=HALVES, i=TILES),
                    in1=recip_all[:].rearrange("p (i h m) -> p i h m", h=HALVES, i=TILES),
                    op=ALU.mult,
                )
                stores.append((g, o_rows))
            for g, o_rows in stores[1:] + stores[:1]:
                nc.sync.dma_start(out=out[b, tile_cols(g), :], in_=o_rows[:])

        steps = (
            (values, 1),
            (exponentials, 1),
            (transpose_q, 0),
            (quantise_last, 2),
            (group_x, 0),
            (widen_q, 0),
            (spread_reciprocals, 2),
            (quantise_x, 0),
            (transpose_e, 1),
            (keep_reciprocals, 2),
            (reciprocal_sums, 1),
            (result, 3),
            (group_e, 1),
            (turn_values, 1),
            (scores, 0),
            (maxima, 0),
        )
        load_x(1)
        load_heads(1)
        for j in range(BATCH + 3):
            if j + 2 < BATCH:
                load_x(j + 2)
                load_heads(j + 2)
            for step, lag in steps:
                if 0 <= j - lag < BATCH and (step, j) != (group_x, 0):
                    step(j - lag)
